import numpy as np
import ml_dtypes


def mxq(x, axis, fmt="e4m3"):
    dtype, down = {"e4m3": (ml_dtypes.float8_e4m3fn, 7), "e5m2": (ml_dtypes.float8_e5m2, 14)}[fmt]
    v = np.moveaxis(np.asarray(x, np.float32).astype(ml_dtypes.bfloat16).astype(np.float64), axis, -1)
    blocks = v.reshape(v.shape[:-1] + (-1, 32))
    amax = np.abs(blocks).max(-1, keepdims=True)
    byte = np.maximum(np.where(amax > 0, np.frexp(amax)[1] - 1 + 127, 0) - down, 1)
    scale = np.exp2(byte - 127.0)
    codes = (blocks / scale).astype(np.float32).astype(dtype).astype(np.float64)
    return np.moveaxis((codes * scale).reshape(v.shape), -1, axis)


WIDE = False


def mx_kscale(k):
    if not WIDE:
        return np.ones(k)
    levels = np.array([10, -10, 5, -5, 0])
    if k % 512:
        return np.exp2(np.random.permutation(np.resize(levels, k // 32))).repeat(32)
    a = np.empty((k // 512, 16))
    for p in range(k // 512):
        a[p, :8] = np.random.permutation(np.resize(levels, 8))
        for g in range(8):
            far = levels[np.abs(levels - a[p, g]) >= 10]
            a[p, g + 8] = far[np.random.randint(len(far))]
    return np.exp2(a.ravel()).repeat(32)


BF16 = ml_dtypes.bfloat16


def bf(x):
    return np.asarray(x, np.float32).astype(BF16)


def f64(x):
    return np.asarray(x).astype(np.float64)


E2M1 = np.array([0.0, 0.5, 1.0, 1.5, 2.0, 3.0, 4.0, 6.0, -0.0, -0.5, -1.0, -1.5, -2.0, -3.0, -4.0, -6.0])


def pack_weight(w, fmt):
    k, n = w.shape
    w = f64(bf(w)).reshape(k // 32, 32, n)
    amax = np.abs(w).max(1)
    if fmt == "e4m3":
        byte = np.frexp(amax)[1] - 1 + 127 - 7
    else:
        mant, ex = np.frexp(amax / 6.0)
        byte = np.where(mant > 0.5, ex, ex - 1) + 127
    byte = np.clip(np.where(amax > 0, byte, 1), 1, 254)
    scaled = (w * np.exp2(127.0 - byte)[:, None, :]).reshape(k, n).astype(np.float32)
    by_word = np.ascontiguousarray(scaled.reshape(k // 512, 128, 4, n).transpose(0, 1, 3, 2))
    if fmt == "e4m3":
        words = by_word.astype(ml_dtypes.float8_e4m3fn).view(np.uint8)
    else:
        c = by_word.astype(ml_dtypes.float4_e2m1fn).view(np.uint8) & 0xF
        words = c[..., 0::2] | (c[..., 1::2] << 4)
    return np.ascontiguousarray(words), np.ascontiguousarray(byte.astype(np.uint8).reshape(k // 512, 16, n))


def unpack_weight(words, scales, fmt):
    g, p, n, _ = words.shape
    if fmt == "e4m3":
        vals = np.ascontiguousarray(words).view(ml_dtypes.float8_e4m3fn).astype(np.float64)
    else:
        nib = np.empty((g, p, n, 4), np.uint8)
        nib[..., 0::2] = words & 0xF
        nib[..., 1::2] = words >> 4
        vals = E2M1[nib]
    vals = vals * np.repeat(np.exp2(scales.astype(np.float64) - 127.0), 8, axis=1)[..., None]
    return vals.transpose(0, 1, 3, 2).reshape(g * 512, n)
def pack4(w):
    words, scales = pack_weight(w, "e2m1")
    return words.reshape(words.shape[0], 128, -1), scales


def unpack4(words, scales):
    return unpack_weight(words.reshape(words.shape[0], 128, -1, 2), scales, "e2m1")


NQ, NK, QS, KS, F, DEG = 1024, 1024, 512, 512, 512, 32
EPS = 1e-5
SLOPE = 0.01


def leaky(v):
    return np.where(v >= 0, v, SLOPE * v)


def draw0():
    s, t = mx_kscale(QS), mx_kscale(F)
    x = bf(np.random.standard_normal((NQ, QS)) * s)
    w1_words, w1_scales = pack4(np.random.standard_normal((QS, F)) / np.sqrt(QS) / s[:, None] * t)
    b1 = bf(np.random.standard_normal(F) * 0.5 * t)
    w2_words, w2_scales = pack4(np.random.standard_normal((F, F)) / np.sqrt(F) / t[:, None])
    return {"x": x,
            "w1_words": w1_words,
            "w1_scales": w1_scales,
            "b1": b1,
            "w2_words": w2_words,
            "w2_scales": w2_scales,
            "b2": bf(np.random.standard_normal(F) * 0.5),
            "gamma": bf(1.0 + 0.1 * np.random.standard_normal(F)),
            "beta": bf(0.1 * np.random.standard_normal(F))}


def core(x, w1_words, w1_scales, b1, w2_words, w2_scales, b2, gamma, beta):
    h = leaky((mxq(f64(x), 1, "e4m3") @ unpack4(w1_words, w1_scales)) + f64(b1))
    h = leaky((mxq(h, 1, "e4m3") @ unpack4(w2_words, w2_scales)) + f64(b2))
    mean = h.mean(axis=0)
    var = h.var(axis=0)
    return f64(gamma) * (h - mean) / np.sqrt(var + EPS) + f64(beta)


def e4m3fn_bytes(y):
    return np.clip(np.asarray(y, np.float64), -448.0, 448.0).astype(np.float32).astype(ml_dtypes.float8_e4m3fn).view(np.uint8)


def e4m3fn_values(b):
    return np.asarray(b, np.uint8).view(ml_dtypes.float8_e4m3fn).astype(np.float64)


def setup_inputs():
    d = draw0()
    x0 = np.asarray(d['x']).astype(np.float64)
    s = (np.max(np.abs(x0), axis=(0,), keepdims=True) / 448.0).astype(np.float32)
    out = {}
    for k, v in d.items():
        if k == 'x':
            out['x_bytes'] = e4m3fn_bytes(x0 / s.astype(np.float64))
            out['x_scale'] = s
        else:
            out[k] = v
    return out


def reference(x_bytes, x_scale, w1_words, w1_scales, b1, w2_words, w2_scales, b2, gamma, beta):
    return core(e4m3fn_values(x_bytes) * x_scale.astype(np.float64), w1_words, w1_scales, b1, w2_words, w2_scales, b2, gamma, beta)

@@ -1,0 +1,293 @@
+from contextlib import ExitStack
+
+import concourse.mybir as mybir
+from concourse.masks import make_identity
+
+NQ, K1, K2, F = 1024, 512, 512, 512
+SLOPE = 0.01
+EPS = 1e-5
+FLOPS = 2 * NQ * K1 * K2 + 2 * NQ * K2 * F
+
+F32 = mybir.dt.float32
+BF16 = mybir.dt.bfloat16
+U32 = mybir.dt.uint32
+I32 = mybir.dt.int32
+U8 = mybir.dt.uint8
+FP8 = mybir.dt.float8_e4m3fn
+FP8X4 = mybir.dt.float8_e4m3fn_x4
+FP4X4 = mybir.dt.float4_e2m1fn_x4
+ALU = mybir.AluOpType
+ACT = mybir.ActivationFunctionType
+
+P = 128
+HALF = 512
+
+
+def tile_attention_prop_pa_w4_kernel(tc, x_bytes, x_scale, w1_words, w1_scales, b1, w2_words, w2_scales, b2, gamma, beta, out):
+    nc = tc.nc
+    with ExitStack() as ctx:
+        one = ctx.enter_context(tc.tile_pool(name="one", bufs=1))
+        ring = ctx.enter_context(tc.tile_pool(name="ring", bufs=2))
+        psum = ctx.enter_context(tc.psum_pool(name="psum", bufs=8))
+
+        w1_raw = one.tile([P, 1024], U8, align_bytes=64)
+        w1_sraw = one.tile([P, 512], U8, align_bytes=64)
+        w1_perm = one.tile([P, 1024], U8, align_bytes=64)
+        w1_sperm = one.tile([P, 512], U8, align_bytes=64)
+        w2_raw = one.tile([P, 1024], U8, align_bytes=64)
+        w2_s = one.tile([P, 512], U8, align_bytes=64)
+        xb = [one.tile([P, 2, K1], U8, align_bytes=64, name="xb%d" % c) for c in range(4)]
+        sc_col = one.tile([P, 4], F32)
+        b1_col = one.tile([P, 4], BF16)
+        crow = one.tile([P, P], BF16)
+        cst = one.tile([P, 12], F32)
+        b2s = one.tile([P, 4], F32)
+        dummy = one.tile([P, 1], F32)
+        ident = one.tile([P, P], F32)
+        identb = one.tile([P, P], BF16)
+        xw = [one.tile([P, K1], BF16, align_bytes=64, name="xw%d" % i) for i in range(8)]
+        xg = [one.tile([P, 256, 4], BF16, align_bytes=64, name="xg%d" % c) for c in range(4)]
+        xq = [one.tile([P, HALF], U32, align_bytes=64, name="xq%d" % h) for h in range(2)]
+        xs = [one.tile([P, HALF], U8, align_bytes=64, name="xs%d" % h) for h in range(2)]
+        v1 = [one.tile([P, 4, HALF], F32, align_bytes=64, name="v1_%d" % h) for h in range(2)]
+        h1 = [one.tile([P, 256, 4], BF16, align_bytes=64, name="h1_%d" % c) for c in range(4)]
+        hq = [one.tile([P, HALF], U32, align_bytes=64, name="hq%d" % h) for h in range(2)]
+        hs = [one.tile([P, HALF], U8, align_bytes=64, name="hs%d" % h) for h in range(2)]
+        cc = [[one.tile([P, HALF], F32, name="cc%d_%d" % (j, h)) for h in range(2)] for j in range(4)]
+        h2 = [one.tile([P, NQ], F32, name="h2_%d" % j) for j in range(4)]
+        y2 = [one.tile([P, NQ], F32, name="y2_%d" % j) for j in range(4)]
+        junk = one.tile([P, NQ], F32)
+        acc = [[one.tile([P, 1], F32, name="acc%d_%d" % (j, h)) for h in range(2)] for j in range(4)]
+        bst = [one.tile([P, 2, 6], F32, name="bst%d" % j) for j in range(4)]
+        mv = [one.tile([P, 2], F32, name="mv%d" % j) for j in range(4)]
+        nmean = [one.tile([P, 1], F32, name="nm%d" % j) for j in range(4)]
+        ssq = [one.tile([P, 1], F32, name="ssq%d" % j) for j in range(4)]
+        rstd = [one.tile([P, 1], F32, name="rstd%d" % j) for j in range(4)]
+        scl = [one.tile([P, 1], F32, name="scl%d" % j) for j in range(4)]
+        shf = [one.tile([P, 1], F32, name="shf%d" % j) for j in range(4)]
+
+        out_v = out.rearrange("(p i) n -> p i n", i=8)
+        x_v = x_bytes.rearrange("(p i) k -> p i k", i=8)
+
+        def bank(dt=F32, cols=512):
+            t = psum.tile([P, cols], dt, name="bank")
+            return t
+
+        def load_scales(dst, src):
+            for q in range(4):
+                nc.sync.dma_start(out=dst[32 * q : 32 * q + 4, :].bitcast(I32), in_=src[0, 4 * q : 4 * q + 4, :].bitcast(I32))
+
+        with tc.manual_schedule():
+            nc.gpsimd.memset(dummy[:], 1.0)
+            nc.gpsimd.memset(w1_sraw[:].bitcast(I32), 0)
+            nc.gpsimd.memset(w2_s[:].bitcast(I32), 0)
+            make_identity(nc, ident[:])
+            nc.gpsimd.memset(crow[:], 0.0)
+            nc.gpsimd.tensor_copy(out=identb[:], in_=ident[:])
+
+            nc.scalar.activation(out=dummy[:], in_=dummy[:], func=ACT.Abs_reciprocal_sqrt)
+
+            nc.sync.dma_start(out=xb[0][:], in_=x_v[:, 0:2, :])
+            nc.sync.dma_start(out=w1_raw[:], in_=w1_words[0])
+            nc.sync.dma_start(out=sc_col[:], in_=x_scale.rearrange("o (p t) -> p (o t)", t=4))
+            for c in range(1, 4):
+                nc.sync.dma_start(out=xb[c][:], in_=x_v[:, 2 * c : 2 * c + 2, :])
+            load_scales(w1_sraw, w1_scales)
+            nc.sync.dma_start(out=b1_col[:], in_=b1.rearrange("(p t) -> p t", t=4))
+            nc.sync.dma_start(out=crow[0:4, :], in_=b2.rearrange("(j p) -> j p", p=P))
+            nc.sync.dma_start(out=crow[4:8, :], in_=gamma.rearrange("(j p) -> j p", p=P))
+            nc.sync.dma_start(out=crow[8:12, :], in_=beta.rearrange("(j p) -> j p", p=P))
+            nc.sync.dma_start(out=w2_raw[:], in_=w2_words[0])
+            load_scales(w2_s, w2_scales)
+
+            def widen_v(i):
+                nc.vector.tensor_copy(out=xw[i][:], in_=xb[i // 2][:, i % 2, :].bitcast(FP8))
+
+            def widen_s(i):
+                nc.scalar.copy(out=xw[i][:], in_=xb[i // 2][:, i % 2, :].bitcast(FP8))
+
+            def turn(c):
+                b = bank()
+                for i in range(2):
+                    words = xw[2 * c + i][:].bitcast(F32)
+                    for u in range(2):
+                        nc.tensor.transpose(b[:, 256 * u + 128 * i : 256 * u + 128 * i + 128], words[:, u::2], ident[:])
+                return b
+
+            def scale_x(c, b):
+                nc.vector.tensor_tensor(
+                    out=xg[c][:].rearrange("p r (u e) -> p r u e", u=2),
+                    in0=b[:].bitcast(BF16).rearrange("p (u r e) -> p r u e", u=2, e=2),
+                    in1=sc_col[:].rearrange("p (o u e) -> p o u e", o=1, u=2).to_broadcast([P, 256, 2, 2]),
+                    op=ALU.mult,
+                )
+
+            def quant_x(c):
+                s = slice(256 * (c % 2), 256 * (c % 2) + 256)
+                nc.vector.quantize_mx(out=xq[c // 2][:, s].bitcast(FP8X4), scales=xs[c // 2][:, s], in_=xg[c][:].rearrange("p r t -> p (r t)"))
+
+            def mm1(h):
+                for t in range(4):
+                    b = bank()
+                    nc.tensor.matmul_mx(
+                        out=b[:],
+                        lhsT=w1_perm[:, 256 * t : 256 * t + 256].bitcast(FP4X4),
+                        lhsT_scale=w1_sperm[:, 128 * t : 128 * t + 128],
+                        rhs=xq[h][:].bitcast(FP8X4),
+                        rhs_scale=xs[h][:],
+                        start=True,
+                        stop=True,
+                    )
+                    nc.scalar.activation(out=v1[h][:, t, :], in_=b[:], func=ACT.Identity, bias=b1_col[:, t : t + 1])
+
+            def leaky1(c):
+                v = v1[c // 2][:, :, 256 * (c % 2) : 256 * (c % 2) + 256].rearrange("p t r -> p r t")
+                nc.vector.scalar_tensor_tensor(out=h1[c][:], in0=v, scalar=SLOPE, in1=v, op0=ALU.mult, op1=ALU.max)
+
+            def quant_h(c):
+                s = slice(256 * (c % 2), 256 * (c % 2) + 256)
+                nc.vector.quantize_mx(out=hq[c // 2][:, s].bitcast(FP8X4), scales=hs[c // 2][:, s], in_=h1[c][:].rearrange("p r t -> p (r t)"))
+
+            def mm2(j, h):
+                b = bank()
+                nc.tensor.matmul_mx(
+                    out=b[:],
+                    lhsT=w2_raw[:, 256 * j : 256 * j + 256].bitcast(FP4X4),
+                    lhsT_scale=w2_s[:, 128 * j : 128 * j + 128],
+                    rhs=hq[h][:].bitcast(FP8X4),
+                    rhs_scale=hs[h][:],
+                    start=True,
+                    stop=True,
+                )
+                return b
+
+            def low2(j, h, b):
+                nc.scalar.activation(out=cc[j][h][:], in_=b[:], func=ACT.Identity, bias=b2s[:, j : j + 1], scale=SLOPE)
+
+            def leaky2(j, h, b, summed=True):
+                kw = {"accum_out": acc[j][h][:]} if summed else {}
+                nc.vector.scalar_tensor_tensor(
+                    out=h2[j][:, HALF * h : HALF * h + HALF], in0=b[:], scalar=cst[:, j : j + 1], in1=cc[j][h][:], op0=ALU.add, op1=ALU.max, **kw
+                )
+
+            def moments(j):
+                nc.gpsimd.tensor_scalar(out=nmean[j][:], in0=acc[j][0][:], scalar1=acc[j][1][:], scalar2=-1.0 / NQ, op0=ALU.add, op1=ALU.mult)
+                nc.scalar.activation(out=junk[:], in_=h2[j][:], func=ACT.Square, bias=nmean[j][:], accum_out=ssq[j][:])
+                nc.scalar.activation(out=rstd[j][:], in_=ssq[j][:], func=ACT.Abs_reciprocal_sqrt, bias=EPS, scale=1.0 / NQ)
+
+            def bn_half(j, h):
+                nc.vector.bn_stats(out=bst[j][:, h, :], in_=h2[j][:, HALF * h : HALF * h + HALF])
+
+            def bn_end(j):
+                nc.vector.bn_aggr(out=mv[j][:], in_=bst[j][:].rearrange("p a b -> p (a b)"))
+                nc.scalar.activation(out=rstd[j][:], in_=mv[j][:, 1:2], func=ACT.Abs_reciprocal_sqrt, bias=EPS)
+                nc.vector.tensor_scalar(out=nmean[j][:], in0=mv[j][:, 0:1], scalar1=-1.0, scalar2=0.0, op0=ALU.mult, op1=ALU.add)
+
+            def affine(j):
+                nc.gpsimd.tensor_tensor(out=scl[j][:], in0=rstd[j][:], in1=cst[:, 4 + j : 5 + j], op=ALU.mult)
+                nc.gpsimd.tensor_scalar(out=shf[j][:], in0=nmean[j][:], scalar1=scl[j][:], scalar2=cst[:, 8 + j : 9 + j], op0=ALU.mult, op1=ALU.add)
+
+            def affine_v(j):
+                nc.vector.tensor_tensor(out=scl[j][:], in0=rstd[j][:], in1=cst[:, 4 + j : 5 + j], op=ALU.mult)
+                nc.vector.tensor_scalar(out=shf[j][:], in0=nmean[j][:], scalar1=scl[j][:], scalar2=cst[:, 8 + j : 9 + j], op0=ALU.mult, op1=ALU.add)
+
+            def norm(eng, j, lo, hi):
+                eng.tensor_scalar(out=y2[j][:, lo:hi], in0=h2[j][:, lo:hi], scalar1=scl[j][:], scalar2=shf[j][:], op0=ALU.mult, op1=ALU.add)
+
+            def flip(j, g):
+                b = bank()
+                for i in range(4):
+                    c0 = 128 * (4 * g + i)
+                    nc.tensor.transpose(b[:, 128 * i : 128 * i + 128], y2[j][:, c0 : c0 + 128], ident[:])
+                return b
+
+            def drain(j, g, b, eng):
+                o = ring.tile([P, 4, P], F32, name="o%d" % (g + 2 * (j % 2)))
+                f = nc.vector.tensor_copy if eng == "v" else nc.scalar.copy
+                f(out=o[:].rearrange("p i n -> p (i n)"), in_=b[:])
+                nc.sync.dma_start(out=out_v[:, 4 * g : 4 * g + 4, 128 * j : 128 * j + 128], in_=o[:])
+
+            widen_v(0)
+            widen_v(1)
+            t0 = turn(0)
+            nc.vector.tensor_copy(
+                out=w1_perm[:].rearrange("p (t m b) -> p t m b", t=4, b=2),
+                in_=w1_raw[:].rearrange("p (m t b) -> p t m b", t=4, b=2),
+            )
+            nc.gpsimd.tensor_copy(
+                out=w1_sperm[:].rearrange("p (t m) -> p t m", t=4),
+                in_=w1_sraw[:].rearrange("p (m t) -> p t m", t=4),
+            )
+            widen_s(2)
+            widen_s(3)
+            t1 = turn(1)
+            scale_x(0, t0)
+            scale_x(1, t1)
+            widen_s(4)
+            widen_s(5)
+            t2 = turn(2)
+            quant_x(0)
+            quant_x(1)
+            widen_s(6)
+            widen_s(7)
+            t3 = turn(3)
+            mm1(0)
+            scale_x(2, t2)
+            scale_x(3, t3)
+            quant_x(2)
+            quant_x(3)
+            cps = bank(BF16, 1024)
+            nc.tensor.transpose(cps[:, 0:128], crow[:], identb[:])
+            nc.vector.tensor_copy(out=cst[:], in_=cps[:, 0:12])
+            nc.gpsimd.tensor_scalar(out=b2s[:], in0=cst[:, 0:4], scalar1=SLOPE, scalar2=0.0, op0=ALU.mult, op1=ALU.add)
+            leaky1(0)
+            leaky1(1)
+            mm1(1)
+            quant_h(0)
+            quant_h(1)
+            ba = [None] * 4
+            for j in range(4):
+                ba[j] = mm2(j, 0)
+                low2(j, 0, ba[j])
+            leaky1(2)
+            leaky1(3)
+            quant_h(2)
+            quant_h(3)
+            bb = [None] * 4
+            leaky2(0, 0, ba[0])
+            leaky2(1, 0, ba[1])
+            for j in range(4):
+                bb[j] = mm2(j, 1)
+                low2(j, 1, bb[j])
+            leaky2(2, 0, ba[2])
+            leaky2(0, 1, bb[0])
+            leaky2(1, 1, bb[1])
+            moments(0)
+            leaky2(3, 0, ba[3], False)
+            leaky2(2, 1, bb[2])
+            moments(1)
+            leaky2(3, 1, bb[3], False)
+            moments(2)
+            affine(0)
+            norm(nc.gpsimd, 0, 0, 512)
+            norm(nc.gpsimd, 0, 512, 1024)
+            bn_half(3, 0)
+            bn_half(3, 1)
+            bn_end(3)
+            drain(0, 0, flip(0, 0), "v")
+            affine_v(3)
+            norm(nc.vector, 3, 0, 512)
+            norm(nc.vector, 3, 512, 1024)
+            affine(1)
+            norm(nc.gpsimd, 1, 0, 512)
+            norm(nc.gpsimd, 1, 512, 1024)
+            drain(0, 1, flip(0, 1), "s")
+            affine_v(2)
+            norm(nc.vector, 2, 0, 512)
+            norm(nc.vector, 2, 512, 1024)
+            drain(3, 0, flip(3, 0), "v")
+            drain(3, 1, flip(3, 1), "s")
+            drain(2, 0, flip(2, 0), "v")
+            drain(1, 0, flip(1, 0), "s")
+            drain(2, 1, flip(2, 1), "v")
+            drain(1, 1, flip(1, 1), "s")

@@ -27,8 +27,7 @@ def tile_attention_prop_pa_w4_kernel(tc, x_bytes, x_scale, w1_words, w1_scales, 
     nc = tc.nc
     with ExitStack() as ctx:
         one = ctx.enter_context(tc.tile_pool(name="one", bufs=1))
-        ring = ctx.enter_context(tc.tile_pool(name="ring", bufs=2))
-        psum = ctx.enter_context(tc.psum_pool(name="psum", bufs=8))
+        psum = ctx.enter_context(tc.psum_pool(name="psum", bufs=1))
 
         w1_raw = one.tile([P, 1024], U8, align_bytes=64)
         w1_sraw = one.tile([P, 512], U8, align_bytes=64)
@@ -49,13 +48,14 @@ def tile_attention_prop_pa_w4_kernel(tc, x_bytes, x_scale, w1_words, w1_scales, 
         xg = [one.tile([P, 256, 4], BF16, align_bytes=64, name="xg%d" % c) for c in range(4)]
         xq = [one.tile([P, HALF], U32, align_bytes=64, name="xq%d" % h) for h in range(2)]
         xs = [one.tile([P, HALF], U8, align_bytes=64, name="xs%d" % h) for h in range(2)]
-        v1 = [one.tile([P, 4, HALF], F32, align_bytes=64, name="v1_%d" % h) for h in range(2)]
+        v1 = [one.tile([P, 4, 256], F32, align_bytes=64, name="v1_%d" % c) for c in range(4)]
         h1 = [one.tile([P, 256, 4], BF16, align_bytes=64, name="h1_%d" % c) for c in range(4)]
         hq = [one.tile([P, HALF], U32, align_bytes=64, name="hq%d" % h) for h in range(2)]
         hs = [one.tile([P, HALF], U8, align_bytes=64, name="hs%d" % h) for h in range(2)]
         cc = [[one.tile([P, HALF], F32, name="cc%d_%d" % (j, h)) for h in range(2)] for j in range(4)]
         h2 = [one.tile([P, NQ], F32, name="h2_%d" % j) for j in range(4)]
         y2 = [one.tile([P, NQ], F32, name="y2_%d" % j) for j in range(4)]
+        ot = [[one.tile([P, 4, P], F32, name="ot%d_%d" % (j, g)) for g in range(2)] for j in range(4)]
         junk = one.tile([P, NQ], F32)
         acc = [[one.tile([P, 1], F32, name="acc%d_%d" % (j, h)) for h in range(2)] for j in range(4)]
         bst = [one.tile([P, 2, 6], F32, name="bst%d" % j) for j in range(4)]
@@ -69,8 +69,8 @@ def tile_attention_prop_pa_w4_kernel(tc, x_bytes, x_scale, w1_words, w1_scales, 
         out_v = out.rearrange("(p i) n -> p i n", i=8)
         x_v = x_bytes.rearrange("(p i) k -> p i k", i=8)
 
-        def bank(dt=F32, cols=512):
-            t = psum.tile([P, cols], dt, name="bank")
+        def bank(k, dt=F32, cols=512):
+            t = psum.tile([P, cols], dt, name="bank%d" % k)
             return t
 
         def load_scales(dst, src):
@@ -89,35 +89,34 @@ def tile_attention_prop_pa_w4_kernel(tc, x_bytes, x_scale, w1_words, w1_scales, 
 
             nc.sync.dma_start(out=xb[0][:], in_=x_v[:, 0:2, :])
             nc.sync.dma_start(out=w1_raw[:], in_=w1_words[0])
-            nc.sync.dma_start(out=sc_col[:], in_=x_scale.rearrange("o (p t) -> p (o t)", t=4))
+            nc.gpsimd.dma_start(out=sc_col[:], in_=x_scale.rearrange("o (p t) -> p (o t)", t=4))
+            nc.gpsimd.dma_start(out=b1_col[:], in_=b1.rearrange("(p t) -> p t", t=4))
             for c in range(1, 4):
                 nc.sync.dma_start(out=xb[c][:], in_=x_v[:, 2 * c : 2 * c + 2, :])
             load_scales(w1_sraw, w1_scales)
-            nc.sync.dma_start(out=b1_col[:], in_=b1.rearrange("(p t) -> p t", t=4))
+            nc.sync.dma_start(out=w2_raw[:], in_=w2_words[0])
             nc.sync.dma_start(out=crow[0:4, :], in_=b2.rearrange("(j p) -> j p", p=P))
             nc.sync.dma_start(out=crow[4:8, :], in_=gamma.rearrange("(j p) -> j p", p=P))
             nc.sync.dma_start(out=crow[8:12, :], in_=beta.rearrange("(j p) -> j p", p=P))
-            nc.sync.dma_start(out=w2_raw[:], in_=w2_words[0])
             load_scales(w2_s, w2_scales)
 
-            def widen_v(i):
-                nc.vector.tensor_copy(out=xw[i][:], in_=xb[i // 2][:, i % 2, :].bitcast(FP8))
+            T = {}
 
-            def widen_s(i):
-                nc.scalar.copy(out=xw[i][:], in_=xb[i // 2][:, i % 2, :].bitcast(FP8))
+            def widen(i, e):
+                (nc.vector.tensor_copy if e == "v" else nc.scalar.copy)(out=xw[i][:], in_=xb[i // 2][:, i % 2, :].bitcast(FP8))
 
             def turn(c):
-                b = bank()
+                b = bank(4 + c)
                 for i in range(2):
                     words = xw[2 * c + i][:].bitcast(F32)
                     for u in range(2):
                         nc.tensor.transpose(b[:, 256 * u + 128 * i : 256 * u + 128 * i + 128], words[:, u::2], ident[:])
-                return b
+                T["x", c] = b
 
-            def scale_x(c, b):
+            def scale_x(c):
                 nc.vector.tensor_tensor(
                     out=xg[c][:].rearrange("p r (u e) -> p r u e", u=2),
-                    in0=b[:].bitcast(BF16).rearrange("p (u r e) -> p r u e", u=2, e=2),
+                    in0=T["x", c][:].bitcast(BF16).rearrange("p (u r e) -> p r u e", u=2, e=2),
                     in1=sc_col[:].rearrange("p (o u e) -> p o u e", o=1, u=2).to_broadcast([P, 256, 2, 2]),
                     op=ALU.mult,
                 )
@@ -126,30 +125,52 @@ def tile_attention_prop_pa_w4_kernel(tc, x_bytes, x_scale, w1_words, w1_scales, 
                 s = slice(256 * (c % 2), 256 * (c % 2) + 256)
                 nc.vector.quantize_mx(out=xq[c // 2][:, s].bitcast(FP8X4), scales=xs[c // 2][:, s], in_=xg[c][:].rearrange("p r t -> p (r t)"))
 
-            def mm1(h):
-                for t in range(4):
-                    b = bank()
-                    nc.tensor.matmul_mx(
-                        out=b[:],
-                        lhsT=w1_perm[:, 256 * t : 256 * t + 256].bitcast(FP4X4),
-                        lhsT_scale=w1_sperm[:, 128 * t : 128 * t + 128],
-                        rhs=xq[h][:].bitcast(FP8X4),
-                        rhs_scale=xs[h][:],
-                        start=True,
-                        stop=True,
-                    )
-                    nc.scalar.activation(out=v1[h][:, t, :], in_=b[:], func=ACT.Identity, bias=b1_col[:, t : t + 1])
+            def perm_w():
+                nc.vector.tensor_copy(
+                    out=w1_perm[:].rearrange("p (t m b) -> p t m b", t=4, b=2),
+                    in_=w1_raw[:].rearrange("p (m t b) -> p t m b", t=4, b=2),
+                )
+
+            def perm_s():
+                nc.gpsimd.tensor_copy(
+                    out=w1_sperm[:].rearrange("p (t m) -> p t m", t=4),
+                    in_=w1_sraw[:].rearrange("p (m t) -> p t m", t=4),
+                )
+
+            def mm1(t, c):
+                if t % 2 == 0:
+                    T["m1", t // 2, c] = bank(2 * c + t // 2)
+                nc.tensor.matmul_mx(
+                    out=T["m1", t // 2, c][:, 256 * (t % 2) : 256 * (t % 2) + 256],
+                    lhsT=w1_perm[:, 256 * t : 256 * t + 256].bitcast(FP4X4),
+                    lhsT_scale=w1_sperm[:, 128 * t : 128 * t + 128],
+                    rhs=xq[c // 2][:, 256 * (c % 2) : 256 * (c % 2) + 256].bitcast(FP8X4),
+                    rhs_scale=xs[c // 2][:, 256 * (c % 2) : 256 * (c % 2) + 256],
+                    start=True,
+                    stop=True,
+                )
+
+            def bias1(t, c):
+                nc.scalar.activation(
+                    out=v1[c][:, t, :], in_=T["m1", t // 2, c][:, 256 * (t % 2) : 256 * (t % 2) + 256], func=ACT.Identity, bias=b1_col[:, t : t + 1]
+                )
 
             def leaky1(c):
-                v = v1[c // 2][:, :, 256 * (c % 2) : 256 * (c % 2) + 256].rearrange("p t r -> p r t")
+                v = v1[c][:].rearrange("p t r -> p r t")
                 nc.vector.scalar_tensor_tensor(out=h1[c][:], in0=v, scalar=SLOPE, in1=v, op0=ALU.mult, op1=ALU.max)
 
             def quant_h(c):
                 s = slice(256 * (c % 2), 256 * (c % 2) + 256)
                 nc.vector.quantize_mx(out=hq[c // 2][:, s].bitcast(FP8X4), scales=hs[c // 2][:, s], in_=h1[c][:].rearrange("p r t -> p (r t)"))
 
+            def vecs():
+                cps = bank(4, BF16, 1024)
+                nc.tensor.transpose(cps[:, 0:128], crow[:], identb[:])
+                nc.vector.tensor_copy(out=cst[:], in_=cps[:, 0:12])
+                nc.gpsimd.tensor_scalar(out=b2s[:], in0=cst[:, 0:4], scalar1=SLOPE, scalar2=0.0, op0=ALU.mult, op1=ALU.add)
+
             def mm2(j, h):
-                b = bank()
+                b = bank(4 * h + j)
                 nc.tensor.matmul_mx(
                     out=b[:],
                     lhsT=w2_raw[:, 256 * j : 256 * j + 256].bitcast(FP4X4),
@@ -159,20 +180,24 @@ def tile_attention_prop_pa_w4_kernel(tc, x_bytes, x_scale, w1_words, w1_scales, 
                     start=True,
                     stop=True,
                 )
-                return b
+                T["m2", j, h] = b
 
-            def low2(j, h, b):
-                nc.scalar.activation(out=cc[j][h][:], in_=b[:], func=ACT.Identity, bias=b2s[:, j : j + 1], scale=SLOPE)
+            def low2(j, h):
+                nc.scalar.activation(out=cc[j][h][:], in_=T["m2", j, h][:], func=ACT.Identity, bias=b2s[:, j : j + 1], scale=SLOPE)
 
-            def leaky2(j, h, b, summed=True):
+            def leaky2(j, h, summed):
                 kw = {"accum_out": acc[j][h][:]} if summed else {}
                 nc.vector.scalar_tensor_tensor(
-                    out=h2[j][:, HALF * h : HALF * h + HALF], in0=b[:], scalar=cst[:, j : j + 1], in1=cc[j][h][:], op0=ALU.add, op1=ALU.max, **kw
+                    out=h2[j][:, HALF * h : HALF * h + HALF], in0=T["m2", j, h][:], scalar=cst[:, j : j + 1], in1=cc[j][h][:], op0=ALU.add, op1=ALU.max, **kw
                 )
 
-            def moments(j):
+            def mean(j):
                 nc.gpsimd.tensor_scalar(out=nmean[j][:], in0=acc[j][0][:], scalar1=acc[j][1][:], scalar2=-1.0 / NQ, op0=ALU.add, op1=ALU.mult)
+
+            def square(j):
                 nc.scalar.activation(out=junk[:], in_=h2[j][:], func=ACT.Square, bias=nmean[j][:], accum_out=ssq[j][:])
+
+            def rstd_s(j):
                 nc.scalar.activation(out=rstd[j][:], in_=ssq[j][:], func=ACT.Abs_reciprocal_sqrt, bias=EPS, scale=1.0 / NQ)
 
             def bn_half(j, h):
@@ -180,114 +205,129 @@ def tile_attention_prop_pa_w4_kernel(tc, x_bytes, x_scale, w1_words, w1_scales, 
 
             def bn_end(j):
                 nc.vector.bn_aggr(out=mv[j][:], in_=bst[j][:].rearrange("p a b -> p (a b)"))
+
+            def bn_neg(j):
+                nc.gpsimd.tensor_scalar(out=nmean[j][:], in0=mv[j][:, 0:1], scalar1=-1.0, scalar2=0.0, op0=ALU.mult, op1=ALU.add)
+
+            def rstd_v(j):
                 nc.scalar.activation(out=rstd[j][:], in_=mv[j][:, 1:2], func=ACT.Abs_reciprocal_sqrt, bias=EPS)
-                nc.vector.tensor_scalar(out=nmean[j][:], in0=mv[j][:, 0:1], scalar1=-1.0, scalar2=0.0, op0=ALU.mult, op1=ALU.add)
 
-            def affine(j):
-                nc.gpsimd.tensor_tensor(out=scl[j][:], in0=rstd[j][:], in1=cst[:, 4 + j : 5 + j], op=ALU.mult)
-                nc.gpsimd.tensor_scalar(out=shf[j][:], in0=nmean[j][:], scalar1=scl[j][:], scalar2=cst[:, 8 + j : 9 + j], op0=ALU.mult, op1=ALU.add)
+            def gain(j, e):
+                (nc.vector if e == "v" else nc.gpsimd).tensor_tensor(out=scl[j][:], in0=rstd[j][:], in1=cst[:, 4 + j : 5 + j], op=ALU.mult)
 
-            def affine_v(j):
-                nc.vector.tensor_tensor(out=scl[j][:], in0=rstd[j][:], in1=cst[:, 4 + j : 5 + j], op=ALU.mult)
-                nc.vector.tensor_scalar(out=shf[j][:], in0=nmean[j][:], scalar1=scl[j][:], scalar2=cst[:, 8 + j : 9 + j], op0=ALU.mult, op1=ALU.add)
+            def shift(j, e):
+                (nc.vector if e == "v" else nc.gpsimd).tensor_scalar(out=shf[j][:], in0=nmean[j][:], scalar1=scl[j][:], scalar2=cst[:, 8 + j : 9 + j], op0=ALU.mult, op1=ALU.add)
 
-            def norm(eng, j, lo, hi):
-                eng.tensor_scalar(out=y2[j][:, lo:hi], in0=h2[j][:, lo:hi], scalar1=scl[j][:], scalar2=shf[j][:], op0=ALU.mult, op1=ALU.add)
+            def norm(j, g, e):
+                lo, hi = 512 * g, 512 * g + 512
+                if e == "s":
+                    nc.scalar.activation(out=y2[j][:, lo:hi], in_=h2[j][:, lo:hi], func=ACT.Identity, scale=scl[j][:], bias=shf[j][:])
+                else:
+                    (nc.vector if e == "v" else nc.gpsimd).tensor_scalar(out=y2[j][:, lo:hi], in0=h2[j][:, lo:hi], scalar1=scl[j][:], scalar2=shf[j][:], op0=ALU.mult, op1=ALU.add)
 
             def flip(j, g):
-                b = bank()
+                b = bank(4 * g + j)
                 for i in range(4):
                     c0 = 128 * (4 * g + i)
                     nc.tensor.transpose(b[:, 128 * i : 128 * i + 128], y2[j][:, c0 : c0 + 128], ident[:])
-                return b
+                T["f", j, g] = b
 
-            def drain(j, g, b, eng):
-                o = ring.tile([P, 4, P], F32, name="o%d" % (g + 2 * (j % 2)))
-                f = nc.vector.tensor_copy if eng == "v" else nc.scalar.copy
-                f(out=o[:].rearrange("p i n -> p (i n)"), in_=b[:])
-                nc.sync.dma_start(out=out_v[:, 4 * g : 4 * g + 4, 128 * j : 128 * j + 128], in_=o[:])
+            def drain(j, g, e):
+                (nc.vector.tensor_copy if e == "v" else nc.scalar.copy)(out=ot[j][g][:].rearrange("p i n -> p (i n)"), in_=T["f", j, g][:])
 
-            widen_v(0)
-            widen_v(1)
-            t0 = turn(0)
-            nc.vector.tensor_copy(
-                out=w1_perm[:].rearrange("p (t m b) -> p t m b", t=4, b=2),
-                in_=w1_raw[:].rearrange("p (m t b) -> p t m b", t=4, b=2),
-            )
-            nc.gpsimd.tensor_copy(
-                out=w1_sperm[:].rearrange("p (t m) -> p t m", t=4),
-                in_=w1_sraw[:].rearrange("p (m t) -> p t m", t=4),
-            )
-            widen_s(2)
-            widen_s(3)
-            t1 = turn(1)
-            scale_x(0, t0)
-            scale_x(1, t1)
-            widen_s(4)
-            widen_s(5)
-            t2 = turn(2)
-            quant_x(0)
-            quant_x(1)
-            widen_s(6)
-            widen_s(7)
-            t3 = turn(3)
-            mm1(0)
-            scale_x(2, t2)
-            scale_x(3, t3)
-            quant_x(2)
-            quant_x(3)
-            cps = bank(BF16, 1024)
-            nc.tensor.transpose(cps[:, 0:128], crow[:], identb[:])
-            nc.vector.tensor_copy(out=cst[:], in_=cps[:, 0:12])
-            nc.gpsimd.tensor_scalar(out=b2s[:], in0=cst[:, 0:4], scalar1=SLOPE, scalar2=0.0, op0=ALU.mult, op1=ALU.add)
-            leaky1(0)
-            leaky1(1)
-            mm1(1)
-            quant_h(0)
-            quant_h(1)
-            ba = [None] * 4
-            for j in range(4):
-                ba[j] = mm2(j, 0)
-                low2(j, 0, ba[j])
-            leaky1(2)
-            leaky1(3)
-            quant_h(2)
-            quant_h(3)
-            bb = [None] * 4
-            leaky2(0, 0, ba[0])
-            leaky2(1, 0, ba[1])
-            for j in range(4):
-                bb[j] = mm2(j, 1)
-                low2(j, 1, bb[j])
-            leaky2(2, 0, ba[2])
-            leaky2(0, 1, bb[0])
-            leaky2(1, 1, bb[1])
-            moments(0)
-            leaky2(3, 0, ba[3], False)
-            leaky2(2, 1, bb[2])
-            moments(1)
-            leaky2(3, 1, bb[3], False)
-            moments(2)
-            affine(0)
-            norm(nc.gpsimd, 0, 0, 512)
-            norm(nc.gpsimd, 0, 512, 1024)
-            bn_half(3, 0)
+            def store(j, g):
+                nc.sync.dma_start(out=out_v[:, 4 * g : 4 * g + 4, 128 * j : 128 * j + 128], in_=ot[j][g][:])
+
+
+            widen(0, "v")
+            widen(1, "s")
+            turn(0)
+            perm_w()
+            perm_s()
+            for c in (1, 2, 3):
+                widen(2 * c, "s")
+                widen(2 * c + 1, "s")
+                turn(c)
+            for h in range(2):
+                for c in (2 * h, 2 * h + 1): scale_x(c)
+                for c in (2 * h, 2 * h + 1): quant_x(c)
+                if h == 1: vecs()
+                for c in (2 * h, 2 * h + 1):
+                    for t in range(4): mm1(t, c)
+                    for t in range(4): bias1(t, c)
+            for h in range(2):
+                for c in (2 * h, 2 * h + 1): leaky1(c)
+                for c in (2 * h, 2 * h + 1): quant_h(c)
+                for j in range(4): mm2(j, h)
+            low2(0, 0)
+            leaky2(0, 0, True)
+            low2(1, 0)
+            leaky2(1, 0, False)
+            low2(2, 0)
+            leaky2(2, 0, True)
+            low2(3, 0)
+            low2(0, 1)
+            leaky2(0, 1, True)
+            low2(1, 1)
+            low2(2, 1)
+            leaky2(1, 1, False)
+            mean(0)
+            square(0)
+            leaky2(2, 1, True)
+            mean(2)
+            rstd_s(0)
+            gain(0, "g")
+            shift(0, "g")
+            bn_half(1, 0)
+            bn_half(1, 1)
+            bn_end(1)
+            low2(3, 1)
+            rstd_v(1)
+            square(2)
+            norm(0, 0, "v")
+            norm(0, 1, "v")
+            flip(0, 0)
+            drain(0, 0, "s")
+            leaky2(3, 1, False)
+            store(0, 0)
+            leaky2(3, 0, False)
+            gain(1, "g")
+            bn_neg(1)
+            shift(1, "g")
             bn_half(3, 1)
+            rstd_s(2)
+            gain(2, "v")
+            bn_half(3, 0)
+            flip(0, 1)
+            drain(0, 1, "s")
+            store(0, 1)
+            shift(2, "v")
+            norm(1, 0, "g")
+            flip(1, 0)
+            drain(1, 0, "s")
+            norm(1, 1, "g")
             bn_end(3)
-            drain(0, 0, flip(0, 0), "v")
-            affine_v(3)
-            norm(nc.vector, 3, 0, 512)
-            norm(nc.vector, 3, 512, 1024)
-            affine(1)
-            norm(nc.gpsimd, 1, 0, 512)
-            norm(nc.gpsimd, 1, 512, 1024)
-            drain(0, 1, flip(0, 1), "s")
-            affine_v(2)
-            norm(nc.vector, 2, 0, 512)
-            norm(nc.vector, 2, 512, 1024)
-            drain(3, 0, flip(3, 0), "v")
-            drain(3, 1, flip(3, 1), "s")
-            drain(2, 0, flip(2, 0), "v")
-            drain(1, 0, flip(1, 0), "s")
-            drain(2, 1, flip(2, 1), "v")
-            drain(1, 1, flip(1, 1), "s")
+            bn_neg(3)
+            store(1, 0)
+            flip(1, 1)
+            norm(2, 0, "v")
+            flip(2, 0)
+            norm(2, 1, "v")
+            rstd_v(3)
+            drain(1, 1, "s")
+            store(1, 1)
+            drain(2, 0, "v")
+            flip(2, 1)
+            drain(2, 1, "s")
+            store(2, 0)
+            store(2, 1)
+            gain(3, "g")
+            shift(3, "g")
+            norm(3, 0, "v")
+            norm(3, 1, "g")
+            flip(3, 1)
+            flip(3, 0)
+            drain(3, 1, "v")
+            drain(3, 0, "s")
+            store(3, 1)
+            store(3, 0)

@@ -49,6 +49,7 @@ def tile_attention_prop_pa_w4_kernel(tc, x_bytes, x_scale, w1_words, w1_scales, 
         xq = [one.tile([P, HALF], U32, align_bytes=64, name="xq%d" % h) for h in range(2)]
         xs = [one.tile([P, HALF], U8, align_bytes=64, name="xs%d" % h) for h in range(2)]
         v1 = [one.tile([P, 4, 256], F32, align_bytes=64, name="v1_%d" % c) for c in range(4)]
+        hp = [one.tile([P, 4, 256], BF16, align_bytes=64, name="hp%d" % c) for c in range(4)]
         h1 = [one.tile([P, 256, 4], BF16, align_bytes=64, name="h1_%d" % c) for c in range(4)]
         hq = [one.tile([P, HALF], U32, align_bytes=64, name="hq%d" % h) for h in range(2)]
         hs = [one.tile([P, HALF], U8, align_bytes=64, name="hs%d" % h) for h in range(2)]
@@ -138,7 +139,7 @@ def tile_attention_prop_pa_w4_kernel(tc, x_bytes, x_scale, w1_words, w1_scales, 
                 )
 
             def mm1(t, c):
-                if t % 2 == 0:
+                if ("m1", t // 2, c) not in T:
                     T["m1", t // 2, c] = bank(2 * c + t // 2)
                 nc.tensor.matmul_mx(
                     out=T["m1", t // 2, c][:, 256 * (t % 2) : 256 * (t % 2) + 256],
@@ -156,8 +157,13 @@ def tile_attention_prop_pa_w4_kernel(tc, x_bytes, x_scale, w1_words, w1_scales, 
                 )
 
             def leaky1(c):
-                v = v1[c][:].rearrange("p t r -> p r t")
-                nc.vector.scalar_tensor_tensor(out=h1[c][:], in0=v, scalar=SLOPE, in1=v, op0=ALU.mult, op1=ALU.max)
+                v = v1[c][:].rearrange("p t r -> p (t r)")
+                nc.vector.scalar_tensor_tensor(out=hp[c][:].rearrange("p t r -> p (t r)"), in0=v, scalar=SLOPE, in1=v, op0=ALU.mult, op1=ALU.max)
+
+            def weave(c, e):
+                (nc.vector.tensor_copy if e == "v" else nc.scalar.copy)(
+                    out=h1[c][:].rearrange("p (b i) t -> p b t i", i=4), in_=hp[c][:].rearrange("p t (b i) -> p b t i", i=4)
+                )
 
             def quant_h(c):
                 s = slice(256 * (c % 2), 256 * (c % 2) + 256)
@@ -248,86 +254,119 @@ def tile_attention_prop_pa_w4_kernel(tc, x_bytes, x_scale, w1_words, w1_scales, 
                 widen(2 * c, "s")
                 widen(2 * c + 1, "s")
                 turn(c)
-            for h in range(2):
-                for c in (2 * h, 2 * h + 1): scale_x(c)
-                for c in (2 * h, 2 * h + 1): quant_x(c)
-                if h == 1: vecs()
-                for c in (2 * h, 2 * h + 1):
-                    for t in range(4): mm1(t, c)
-                    for t in range(4): bias1(t, c)
-            for h in range(2):
-                for c in (2 * h, 2 * h + 1): leaky1(c)
-                for c in (2 * h, 2 * h + 1): quant_h(c)
-                for j in range(4): mm2(j, h)
-            low2(0, 0)
-            leaky2(0, 0, True)
-            low2(1, 0)
-            leaky2(1, 0, False)
+            for c in (0, 1): scale_x(c)
+            for c in (0, 1): quant_x(c)
+            for c in (0, 1):
+                for t in range(4): mm1(t, c)
+                for t in range(4): bias1(t, c)
+            for c in (2, 3): scale_x(c)
+            for c in (2, 3): quant_x(c)
+            mm1(3, 2)
+            leaky1(0)
+            vecs()
+            mm1(2, 2)
+            bias1(3, 2)
+            mm1(0, 3)
+            bias1(2, 2)
+            mm1(1, 3)
+            bias1(1, 3)
+            mm1(3, 3)
+            bias1(3, 3)
+            leaky1(1)
+            mm1(0, 2)
+            mm1(1, 2)
+            bias1(0, 2)
+            weave(0, "v")
+            bias1(1, 2)
+            mm1(2, 3)
+            weave(1, "s")
+            leaky1(2)
+            bias1(0, 3)
+            quant_h(1)
+            bias1(2, 3)
+            quant_h(0)
+            mm2(2, 0)
+            weave(2, "s")
+            leaky1(3)
+            weave(3, "v")
+            mm2(3, 0)
             low2(2, 0)
-            leaky2(2, 0, True)
+            mm2(0, 0)
+            quant_h(2)
+            quant_h(3)
             low2(3, 0)
+            mm2(1, 0)
+            low2(0, 0)
+            leaky2(2, 0, False)
+            mm2(0, 1)
+            leaky2(0, 0, True)
+            bn_half(2, 0)
+            low2(1, 0)
+            mm2(1, 1)
             low2(0, 1)
-            leaky2(0, 1, True)
             low2(1, 1)
+            leaky2(0, 1, True)
+            mm2(2, 1)
+            leaky2(1, 1, True)
+            leaky2(1, 0, True)
             low2(2, 1)
-            leaky2(1, 1, False)
+            leaky2(2, 1, False)
+            bn_half(2, 1)
+            bn_end(2)
             mean(0)
             square(0)
-            leaky2(2, 1, True)
-            mean(2)
             rstd_s(0)
+            mean(1)
+            square(1)
             gain(0, "g")
+            rstd_v(2)
             shift(0, "g")
-            bn_half(1, 0)
-            bn_half(1, 1)
-            bn_end(1)
-            low2(3, 1)
-            rstd_v(1)
-            square(2)
             norm(0, 0, "v")
+            mm2(3, 1)
             norm(0, 1, "v")
+            rstd_s(1)
             flip(0, 0)
+            low2(3, 1)
             drain(0, 0, "s")
-            leaky2(3, 1, False)
+            gain(2, "g")
+            bn_neg(2)
+            gain(1, "v")
+            shift(1, "v")
+            norm(1, 1, "g")
             store(0, 0)
-            leaky2(3, 0, False)
-            gain(1, "g")
-            bn_neg(1)
-            shift(1, "g")
-            bn_half(3, 1)
-            rstd_s(2)
-            gain(2, "v")
-            bn_half(3, 0)
             flip(0, 1)
             drain(0, 1, "s")
+            leaky2(3, 0, False)
+            shift(2, "g")
+            leaky2(3, 1, False)
+            norm(2, 0, "g")
+            flip(1, 1)
             store(0, 1)
-            shift(2, "v")
-            norm(1, 0, "g")
-            flip(1, 0)
-            drain(1, 0, "s")
-            norm(1, 1, "g")
+            norm(2, 1, "g")
+            bn_half(3, 1)
+            drain(1, 1, "s")
+            bn_half(3, 0)
             bn_end(3)
             bn_neg(3)
-            store(1, 0)
-            flip(1, 1)
-            norm(2, 0, "v")
+            norm(1, 0, "s")
             flip(2, 0)
-            norm(2, 1, "v")
-            rstd_v(3)
-            drain(1, 1, "s")
-            store(1, 1)
             drain(2, 0, "v")
+            rstd_v(3)
+            gain(3, "v")
+            store(1, 1)
             flip(2, 1)
             drain(2, 1, "s")
+            flip(1, 0)
+            shift(3, "v")
             store(2, 0)
+            drain(1, 0, "s")
             store(2, 1)
-            gain(3, "g")
-            shift(3, "g")
             norm(3, 0, "v")
             norm(3, 1, "g")
-            flip(3, 1)
             flip(3, 0)
-            drain(3, 1, "v")
             drain(3, 0, "s")
-            store(3, 1)
+            store(1, 0)
+            flip(3, 1)
+            drain(3, 1, "s")
             store(3, 0)
+            store(3, 1)

@@ -35,7 +35,7 @@ def tile_attention_prop_pa_w4_kernel(tc, x_bytes, x_scale, w1_words, w1_scales, 
         w1_sperm = one.tile([P, 512], U8, align_bytes=64)
         w2_raw = one.tile([P, 1024], U8, align_bytes=64)
         w2_s = one.tile([P, 512], U8, align_bytes=64)
-        xb = [one.tile([P, 2, K1], U8, align_bytes=64, name="xb%d" % c) for c in range(4)]
+        xb = [one.tile([P, n, K1], U8, align_bytes=64, name="xb%d" % c) for c, n in enumerate((2, 6))]
         sc_col = one.tile([P, 4], F32)
         b1_col = one.tile([P, 4], BF16)
         crow = one.tile([P, P], BF16)
@@ -49,18 +49,15 @@ def tile_attention_prop_pa_w4_kernel(tc, x_bytes, x_scale, w1_words, w1_scales, 
         xq = [one.tile([P, HALF], U32, align_bytes=64, name="xq%d" % h) for h in range(2)]
         xs = [one.tile([P, HALF], U8, align_bytes=64, name="xs%d" % h) for h in range(2)]
         v1 = [one.tile([P, 4, 256], F32, align_bytes=64, name="v1_%d" % c) for c in range(4)]
-        hp = [one.tile([P, 4, 256], BF16, align_bytes=64, name="hp%d" % c) for c in range(4)]
         h1 = [one.tile([P, 256, 4], BF16, align_bytes=64, name="h1_%d" % c) for c in range(4)]
         hq = [one.tile([P, HALF], U32, align_bytes=64, name="hq%d" % h) for h in range(2)]
         hs = [one.tile([P, HALF], U8, align_bytes=64, name="hs%d" % h) for h in range(2)]
         cc = [[one.tile([P, HALF], F32, name="cc%d_%d" % (j, h)) for h in range(2)] for j in range(4)]
         h2 = [one.tile([P, NQ], F32, name="h2_%d" % j) for j in range(4)]
         y2 = [one.tile([P, NQ], F32, name="y2_%d" % j) for j in range(4)]
-        ot = [[one.tile([P, 4, P], F32, name="ot%d_%d" % (j, g)) for g in range(2)] for j in range(4)]
+        ot = [[one.tile([P, 2, 256], F32, name="ot%d_%d" % (a, q)) for q in range(4)] for a in range(2)]
         junk = one.tile([P, NQ], F32)
         acc = [[one.tile([P, 1], F32, name="acc%d_%d" % (j, h)) for h in range(2)] for j in range(4)]
-        bst = [one.tile([P, 2, 6], F32, name="bst%d" % j) for j in range(4)]
-        mv = [one.tile([P, 2], F32, name="mv%d" % j) for j in range(4)]
         nmean = [one.tile([P, 1], F32, name="nm%d" % j) for j in range(4)]
         ssq = [one.tile([P, 1], F32, name="ssq%d" % j) for j in range(4)]
         rstd = [one.tile([P, 1], F32, name="rstd%d" % j) for j in range(4)]
@@ -86,25 +83,23 @@ def tile_attention_prop_pa_w4_kernel(tc, x_bytes, x_scale, w1_words, w1_scales, 
             nc.gpsimd.memset(crow[:], 0.0)
             nc.gpsimd.tensor_copy(out=identb[:], in_=ident[:])
 
+            nc.scalar.dma_start(out=sc_col[:], in_=x_scale.rearrange("o (p t) -> p (o t)", t=4))
             nc.scalar.activation(out=dummy[:], in_=dummy[:], func=ACT.Abs_reciprocal_sqrt)
-
             nc.sync.dma_start(out=xb[0][:], in_=x_v[:, 0:2, :])
             nc.sync.dma_start(out=w1_raw[:], in_=w1_words[0])
-            nc.gpsimd.dma_start(out=sc_col[:], in_=x_scale.rearrange("o (p t) -> p (o t)", t=4))
-            nc.gpsimd.dma_start(out=b1_col[:], in_=b1.rearrange("(p t) -> p t", t=4))
-            for c in range(1, 4):
-                nc.sync.dma_start(out=xb[c][:], in_=x_v[:, 2 * c : 2 * c + 2, :])
+            nc.sync.dma_start(out=xb[1][:], in_=x_v[:, 2:8, :])
             load_scales(w1_sraw, w1_scales)
-            nc.sync.dma_start(out=w2_raw[:], in_=w2_words[0])
+            nc.sync.dma_start(out=b1_col[:], in_=b1.rearrange("(p t) -> p t", t=4))
             nc.sync.dma_start(out=crow[0:4, :], in_=b2.rearrange("(j p) -> j p", p=P))
             nc.sync.dma_start(out=crow[4:8, :], in_=gamma.rearrange("(j p) -> j p", p=P))
             nc.sync.dma_start(out=crow[8:12, :], in_=beta.rearrange("(j p) -> j p", p=P))
+            nc.sync.dma_start(out=w2_raw[:], in_=w2_words[0])
             load_scales(w2_s, w2_scales)
 
             T = {}
 
             def widen(i, e):
-                (nc.vector.tensor_copy if e == "v" else nc.scalar.copy)(out=xw[i][:], in_=xb[i // 2][:, i % 2, :].bitcast(FP8))
+                (nc.vector.tensor_copy if e == "v" else nc.scalar.copy)(out=xw[i][:], in_=xb[min(i // 2, 1)][:, i - 2 * min(i // 2, 1), :].bitcast(FP8))
 
             def turn(c):
                 b = bank(4 + c)
@@ -132,8 +127,8 @@ def tile_attention_prop_pa_w4_kernel(tc, x_bytes, x_scale, w1_words, w1_scales, 
                     in_=w1_raw[:].rearrange("p (m t b) -> p t m b", t=4, b=2),
                 )
 
-            def perm_s():
-                nc.gpsimd.tensor_copy(
+            def perm_s(e):
+                (nc.vector if e == "v" else nc.gpsimd).tensor_copy(
                     out=w1_sperm[:].rearrange("p (t m) -> p t m", t=4),
                     in_=w1_sraw[:].rearrange("p (m t) -> p t m", t=4),
                 )
@@ -156,23 +151,20 @@ def tile_attention_prop_pa_w4_kernel(tc, x_bytes, x_scale, w1_words, w1_scales, 
                     out=v1[c][:, t, :], in_=T["m1", t // 2, c][:, 256 * (t % 2) : 256 * (t % 2) + 256], func=ACT.Identity, bias=b1_col[:, t : t + 1]
                 )
 
-            def leaky1(c):
-                v = v1[c][:].rearrange("p t r -> p (t r)")
-                nc.vector.scalar_tensor_tensor(out=hp[c][:].rearrange("p t r -> p (t r)"), in0=v, scalar=SLOPE, in1=v, op0=ALU.mult, op1=ALU.max)
-
-            def weave(c, e):
-                (nc.vector.tensor_copy if e == "v" else nc.scalar.copy)(
-                    out=h1[c][:].rearrange("p (b i) t -> p b t i", i=4), in_=hp[c][:].rearrange("p t (b i) -> p b t i", i=4)
-                )
+            def leaky1d(c):
+                v = v1[c][:].rearrange("p t r -> p r t")
+                nc.vector.scalar_tensor_tensor(out=h1[c][:], in0=v, scalar=SLOPE, in1=v, op0=ALU.mult, op1=ALU.max)
 
             def quant_h(c):
                 s = slice(256 * (c % 2), 256 * (c % 2) + 256)
                 nc.vector.quantize_mx(out=hq[c // 2][:, s].bitcast(FP8X4), scales=hs[c // 2][:, s], in_=h1[c][:].rearrange("p r t -> p (r t)"))
 
-            def vecs():
-                cps = bank(4, BF16, 1024)
-                nc.tensor.transpose(cps[:, 0:128], crow[:], identb[:])
-                nc.vector.tensor_copy(out=cst[:], in_=cps[:, 0:12])
+            def vec_turn():
+                T["vec"] = bank(4, BF16, 1024)
+                nc.tensor.transpose(T["vec"][:, 0:128], crow[:], identb[:])
+
+            def vec_copy():
+                nc.vector.tensor_copy(out=cst[:], in_=T["vec"][:, 0:12])
                 nc.gpsimd.tensor_scalar(out=b2s[:], in0=cst[:, 0:4], scalar1=SLOPE, scalar2=0.0, op0=ALU.mult, op1=ALU.add)
 
             def mm2(j, h):
@@ -191,10 +183,9 @@ def tile_attention_prop_pa_w4_kernel(tc, x_bytes, x_scale, w1_words, w1_scales, 
             def low2(j, h):
                 nc.scalar.activation(out=cc[j][h][:], in_=T["m2", j, h][:], func=ACT.Identity, bias=b2s[:, j : j + 1], scale=SLOPE)
 
-            def leaky2(j, h, summed):
-                kw = {"accum_out": acc[j][h][:]} if summed else {}
+            def leaky2(j, h):
                 nc.vector.scalar_tensor_tensor(
-                    out=h2[j][:, HALF * h : HALF * h + HALF], in0=T["m2", j, h][:], scalar=cst[:, j : j + 1], in1=cc[j][h][:], op0=ALU.add, op1=ALU.max, **kw
+                    out=h2[j][:, HALF * h : HALF * h + HALF], in0=T["m2", j, h][:], scalar=cst[:, j : j + 1], in1=cc[j][h][:], op0=ALU.add, op1=ALU.max, accum_out=acc[j][h][:]
                 )
 
             def mean(j):
@@ -205,18 +196,6 @@ def tile_attention_prop_pa_w4_kernel(tc, x_bytes, x_scale, w1_words, w1_scales, 
 
             def rstd_s(j):
                 nc.scalar.activation(out=rstd[j][:], in_=ssq[j][:], func=ACT.Abs_reciprocal_sqrt, bias=EPS, scale=1.0 / NQ)
-
-            def bn_half(j, h):
-                nc.vector.bn_stats(out=bst[j][:, h, :], in_=h2[j][:, HALF * h : HALF * h + HALF])
-
-            def bn_end(j):
-                nc.vector.bn_aggr(out=mv[j][:], in_=bst[j][:].rearrange("p a b -> p (a b)"))
-
-            def bn_neg(j):
-                nc.gpsimd.tensor_scalar(out=nmean[j][:], in0=mv[j][:, 0:1], scalar1=-1.0, scalar2=0.0, op0=ALU.mult, op1=ALU.add)
-
-            def rstd_v(j):
-                nc.scalar.activation(out=rstd[j][:], in_=mv[j][:, 1:2], func=ACT.Abs_reciprocal_sqrt, bias=EPS)
 
             def gain(j, e):
                 (nc.vector if e == "v" else nc.gpsimd).tensor_tensor(out=scl[j][:], in0=rstd[j][:], in1=cst[:, 4 + j : 5 + j], op=ALU.mult)
@@ -231,142 +210,158 @@ def tile_attention_prop_pa_w4_kernel(tc, x_bytes, x_scale, w1_words, w1_scales, 
                 else:
                     (nc.vector if e == "v" else nc.gpsimd).tensor_scalar(out=y2[j][:, lo:hi], in0=h2[j][:, lo:hi], scalar1=scl[j][:], scalar2=shf[j][:], op0=ALU.mult, op1=ALU.add)
 
-            def flip(j, g):
-                b = bank(4 * g + j)
-                for i in range(4):
-                    c0 = 128 * (4 * g + i)
-                    nc.tensor.transpose(b[:, 128 * i : 128 * i + 128], y2[j][:, c0 : c0 + 128], ident[:])
-                T["f", j, g] = b
+            def flip(a, q):
+                b = bank((2 * a, 2 * a + 1, 4 + 2 * a, 5 + 2 * a)[q])
+                for i in range(2):
+                    for n in range(2):
+                        c0 = 128 * (2 * q + i)
+                        nc.tensor.transpose(b[:, 256 * i + 128 * n : 256 * i + 128 * n + 128], y2[2 * a + n][:, c0 : c0 + 128], ident[:])
+                T["f", a, q] = b
 
-            def drain(j, g, e):
-                (nc.vector.tensor_copy if e == "v" else nc.scalar.copy)(out=ot[j][g][:].rearrange("p i n -> p (i n)"), in_=T["f", j, g][:])
+            def drain(a, q, e):
+                (nc.vector.tensor_copy if e == "v" else nc.scalar.copy)(out=ot[a][q][:].rearrange("p i n -> p (i n)"), in_=T["f", a, q][:])
 
-            def store(j, g):
-                nc.sync.dma_start(out=out_v[:, 4 * g : 4 * g + 4, 128 * j : 128 * j + 128], in_=ot[j][g][:])
+            def store(a, q):
+                nc.sync.dma_start(out=out_v[:, 2 * q : 2 * q + 2, 256 * a : 256 * a + 256], in_=ot[a][q][:])
 
 
             widen(0, "v")
             widen(1, "s")
             turn(0)
             perm_w()
-            perm_s()
-            for c in (1, 2, 3):
-                widen(2 * c, "s")
-                widen(2 * c + 1, "s")
-                turn(c)
-            for c in (0, 1): scale_x(c)
-            for c in (0, 1): quant_x(c)
-            for c in (0, 1):
-                for t in range(4): mm1(t, c)
-                for t in range(4): bias1(t, c)
-            for c in (2, 3): scale_x(c)
-            for c in (2, 3): quant_x(c)
-            mm1(3, 2)
-            leaky1(0)
-            vecs()
-            mm1(2, 2)
-            bias1(3, 2)
-            mm1(0, 3)
-            bias1(2, 2)
-            mm1(1, 3)
-            bias1(1, 3)
-            mm1(3, 3)
-            bias1(3, 3)
-            leaky1(1)
-            mm1(0, 2)
-            mm1(1, 2)
-            bias1(0, 2)
-            weave(0, "v")
-            bias1(1, 2)
+            widen(2, "s")
+            widen(3, "s")
+            turn(1)
+            scale_x(0)
+            perm_s("v")
+            quant_x(0)
+            scale_x(1)
+            widen(6, "s")
+            widen(7, "s")
+            turn(3)
+            widen(4, "s")
+            mm1(2, 0)
+            widen(5, "s")
+            turn(2)
+            mm1(3, 0)
+            bias1(3, 0)
+            scale_x(3)
+            quant_x(1)
+            mm1(0, 0)
+            mm1(1, 0)
+            bias1(1, 0)
+            mm1(3, 1)
+            scale_x(2)
+            mm1(2, 1)
+            bias1(0, 0)
+            mm1(0, 1)
+            mm1(1, 1)
+            vec_turn()
+            quant_x(3)
+            bias1(2, 0)
             mm1(2, 3)
-            weave(1, "s")
-            leaky1(2)
-            bias1(0, 3)
-            quant_h(1)
-            bias1(2, 3)
+            quant_x(2)
+            vec_copy()
+            mm1(3, 2)
+            leaky1d(0)
+            bias1(0, 1)
+            bias1(2, 1)
+            mm1(0, 2)
+            mm1(1, 3)
+            bias1(1, 1)
+            bias1(3, 1)
+            leaky1d(1)
+            mm1(1, 2)
+            bias1(1, 2)
+            bias1(0, 2)
+            mm1(2, 2)
+            bias1(2, 2)
+            mm1(0, 3)
             quant_h(0)
+            bias1(1, 3)
+            quant_h(1)
+            bias1(3, 2)
+            bias1(0, 3)
+            leaky1d(2)
+            mm1(3, 3)
             mm2(2, 0)
-            weave(2, "s")
-            leaky1(3)
-            weave(3, "v")
-            mm2(3, 0)
+            bias1(3, 3)
+            bias1(2, 3)
             low2(2, 0)
-            mm2(0, 0)
+            leaky1d(3)
             quant_h(2)
             quant_h(3)
-            low2(3, 0)
+            mm2(0, 0)
             mm2(1, 0)
+            leaky2(2, 0)
             low2(0, 0)
-            leaky2(2, 0, False)
-            mm2(0, 1)
-            leaky2(0, 0, True)
-            bn_half(2, 0)
+            leaky2(0, 0)
+            mm2(3, 0)
+            low2(3, 0)
             low2(1, 0)
-            mm2(1, 1)
+            leaky2(1, 0)
+            mm2(0, 1)
             low2(0, 1)
-            low2(1, 1)
-            leaky2(0, 1, True)
-            mm2(2, 1)
-            leaky2(1, 1, True)
-            leaky2(1, 0, True)
-            low2(2, 1)
-            leaky2(2, 1, False)
-            bn_half(2, 1)
-            bn_end(2)
-            mean(0)
-            square(0)
-            rstd_s(0)
-            mean(1)
-            square(1)
-            gain(0, "g")
-            rstd_v(2)
-            shift(0, "g")
-            norm(0, 0, "v")
             mm2(3, 1)
-            norm(0, 1, "v")
-            rstd_s(1)
-            flip(0, 0)
+            leaky2(0, 1)
+            mm2(2, 1)
             low2(3, 1)
-            drain(0, 0, "s")
-            gain(2, "g")
-            bn_neg(2)
+            mm2(1, 1)
+            low2(2, 1)
+            mean(0)
+            leaky2(3, 1)
+            low2(1, 1)
+            square(0)
+            leaky2(1, 1)
+            mean(1)
+            leaky2(2, 1)
+            rstd_s(0)
+            gain(0, "g")
+            mean(2)
+            leaky2(3, 0)
+            square(1)
+            shift(0, "g")
+            rstd_s(1)
             gain(1, "v")
+            norm(0, 0, "g")
+            mean(3)
             shift(1, "v")
-            norm(1, 1, "g")
-            store(0, 0)
+            norm(1, 0, "v")
+            flip(0, 0)
+            norm(1, 1, "v")
+            square(2)
+            rstd_s(2)
             flip(0, 1)
-            drain(0, 1, "s")
-            leaky2(3, 0, False)
-            shift(2, "g")
-            leaky2(3, 1, False)
-            norm(2, 0, "g")
-            flip(1, 1)
-            store(0, 1)
-            norm(2, 1, "g")
-            bn_half(3, 1)
-            drain(1, 1, "s")
-            bn_half(3, 0)
-            bn_end(3)
-            bn_neg(3)
-            norm(1, 0, "s")
-            flip(2, 0)
-            drain(2, 0, "v")
-            rstd_v(3)
+            gain(2, "g")
+            norm(0, 1, "v")
+            drain(0, 0, "v")
+            store(0, 0)
+            drain(0, 1, "v")
+            square(3)
+            rstd_s(3)
             gain(3, "v")
-            store(1, 1)
-            flip(2, 1)
-            drain(2, 1, "s")
-            flip(1, 0)
+            store(0, 1)
             shift(3, "v")
-            store(2, 0)
-            drain(1, 0, "s")
-            store(2, 1)
+            flip(0, 2)
+            drain(0, 2, "s")
             norm(3, 0, "v")
-            norm(3, 1, "g")
-            flip(3, 0)
-            drain(3, 0, "s")
+            shift(2, "g")
+            norm(2, 0, "g")
+            store(0, 2)
+            norm(2, 1, "v")
+            norm(3, 1, "v")
+            flip(0, 3)
+            flip(1, 0)
+            drain(1, 0, "v")
+            flip(1, 3)
+            drain(1, 3, "v")
+            drain(0, 3, "s")
+            store(0, 3)
+            flip(1, 2)
+            drain(1, 2, "v")
             store(1, 0)
-            flip(3, 1)
-            drain(3, 1, "s")
-            store(3, 0)
-            store(3, 1)
+            store(1, 3)
+            store(1, 2)
+            flip(1, 1)
+            drain(1, 1, "s")
+            store(1, 1)

from contextlib import ExitStack

import concourse.mybir as mybir
from concourse.masks import make_identity

NQ, K1, K2, F = 1024, 512, 512, 512
SLOPE = 0.01
EPS = 1e-5
FLOPS = 2 * NQ * K1 * K2 + 2 * NQ * K2 * F

F32 = mybir.dt.float32
BF16 = mybir.dt.bfloat16
U32 = mybir.dt.uint32
I32 = mybir.dt.int32
U8 = mybir.dt.uint8
FP8 = mybir.dt.float8_e4m3fn
FP8X4 = mybir.dt.float8_e4m3fn_x4
FP4X4 = mybir.dt.float4_e2m1fn_x4
ALU = mybir.AluOpType
ACT = mybir.ActivationFunctionType

P = 128
HALF = 512


def tile_attention_prop_pa_w4_kernel(tc, x_bytes, x_scale, w1_words, w1_scales, b1, w2_words, w2_scales, b2, gamma, beta, out):
    nc = tc.nc
    with ExitStack() as ctx:
        one = ctx.enter_context(tc.tile_pool(name="one", bufs=1))
        psum = ctx.enter_context(tc.psum_pool(name="psum", bufs=1))

        w1_raw = one.tile([P, 1024], U8, align_bytes=64)
        w1_sraw = one.tile([P, 512], U8, align_bytes=64)
        w1_perm = one.tile([P, 1024], U8, align_bytes=64)
        w1_sperm = one.tile([P, 512], U8, align_bytes=64)
        w2_raw = one.tile([P, 1024], U8, align_bytes=64)
        w2_s = one.tile([P, 512], U8, align_bytes=64)
        xb = [one.tile([P, n, K1], U8, align_bytes=64, name="xb%d" % c) for c, n in enumerate((2, 6))]
        sc_col = one.tile([P, 4], F32)
        b1_col = one.tile([P, 4], BF16)
        crow = one.tile([P, P], BF16)
        cst = one.tile([P, 12], F32)
        b2s = one.tile([P, 4], F32)
        dummy = one.tile([P, 1], F32)
        ident = one.tile([P, P], F32)
        identb = one.tile([P, P], BF16)
        xw = [one.tile([P, K1], BF16, align_bytes=64, name="xw%d" % i) for i in range(8)]
        xg = [one.tile([P, 256, 4], BF16, align_bytes=64, name="xg%d" % c) for c in range(4)]
        xq = [one.tile([P, HALF], U32, align_bytes=64, name="xq%d" % h) for h in range(2)]
        xs = [one.tile([P, HALF], U8, align_bytes=64, name="xs%d" % h) for h in range(2)]
        v1 = [one.tile([P, 4, 256], F32, align_bytes=64, name="v1_%d" % c) for c in range(4)]
        h1 = [one.tile([P, 256, 4], BF16, align_bytes=64, name="h1_%d" % c) for c in range(4)]
        hq = [one.tile([P, HALF], U32, align_bytes=64, name="hq%d" % h) for h in range(2)]
        hs = [one.tile([P, HALF], U8, align_bytes=64, name="hs%d" % h) for h in range(2)]
        cc = [[one.tile([P, HALF], F32, name="cc%d_%d" % (j, h)) for h in range(2)] for j in range(4)]
        h2 = [one.tile([P, NQ], F32, name="h2_%d" % j) for j in range(4)]
        y2 = [one.tile([P, NQ], F32, name="y2_%d" % j) for j in range(4)]
        ot = [[one.tile([P, 2, 256], F32, name="ot%d_%d" % (a, q)) for q in range(4)] for a in range(2)]
        junk = one.tile([P, NQ], F32)
        acc = [[one.tile([P, 1], F32, name="acc%d_%d" % (j, h)) for h in range(2)] for j in range(4)]
        nmean = [one.tile([P, 1], F32, name="nm%d" % j) for j in range(4)]
        ssq = [one.tile([P, 1], F32, name="ssq%d" % j) for j in range(4)]
        rstd = [one.tile([P, 1], F32, name="rstd%d" % j) for j in range(4)]
        scl = [one.tile([P, 1], F32, name="scl%d" % j) for j in range(4)]
        shf = [one.tile([P, 1], F32, name="shf%d" % j) for j in range(4)]

        out_v = out.rearrange("(p i) n -> p i n", i=8)
        x_v = x_bytes.rearrange("(p i) k -> p i k", i=8)

        def bank(k, dt=F32, cols=512):
            t = psum.tile([P, cols], dt, name="bank%d" % k)
            return t

        def load_scales(dst, src):
            for q in range(4):
                nc.sync.dma_start(out=dst[32 * q : 32 * q + 4, :].bitcast(I32), in_=src[0, 4 * q : 4 * q + 4, :].bitcast(I32))

        with tc.manual_schedule():
            nc.gpsimd.memset(dummy[:], 1.0)
            nc.gpsimd.memset(w1_sraw[:].bitcast(I32), 0)
            nc.gpsimd.memset(w2_s[:].bitcast(I32), 0)
            make_identity(nc, ident[:])
            nc.gpsimd.memset(crow[:], 0.0)
            nc.gpsimd.tensor_copy(out=identb[:], in_=ident[:])

            nc.scalar.dma_start(out=sc_col[:], in_=x_scale.rearrange("o (p t) -> p (o t)", t=4))
            nc.scalar.activation(out=dummy[:], in_=dummy[:], func=ACT.Abs_reciprocal_sqrt)
            nc.sync.dma_start(out=xb[0][:], in_=x_v[:, 0:2, :])
            nc.sync.dma_start(out=w1_raw[:], in_=w1_words[0])
            nc.sync.dma_start(out=xb[1][:], in_=x_v[:, 2:8, :])
            load_scales(w1_sraw, w1_scales)
            nc.sync.dma_start(out=b1_col[:], in_=b1.rearrange("(p t) -> p t", t=4))
            nc.sync.dma_start(out=crow[0:4, :], in_=b2.rearrange("(j p) -> j p", p=P))
            nc.sync.dma_start(out=crow[4:8, :], in_=gamma.rearrange("(j p) -> j p", p=P))
            nc.sync.dma_start(out=crow[8:12, :], in_=beta.rearrange("(j p) -> j p", p=P))
            nc.sync.dma_start(out=w2_raw[:], in_=w2_words[0])
            load_scales(w2_s, w2_scales)

            T = {}

            def widen(i, e):
                (nc.vector.tensor_copy if e == "v" else nc.scalar.copy)(out=xw[i][:], in_=xb[min(i // 2, 1)][:, i - 2 * min(i // 2, 1), :].bitcast(FP8))

            def turn(c):
                b = bank(4 + c)
                for i in range(2):
                    words = xw[2 * c + i][:].bitcast(F32)
                    for u in range(2):
                        nc.tensor.transpose(b[:, 256 * u + 128 * i : 256 * u + 128 * i + 128], words[:, u::2], ident[:])
                T["x", c] = b

            def scale_x(c):
                nc.vector.tensor_tensor(
                    out=xg[c][:].rearrange("p r (u e) -> p r u e", u=2),
                    in0=T["x", c][:].bitcast(BF16).rearrange("p (u r e) -> p r u e", u=2, e=2),
                    in1=sc_col[:].rearrange("p (o u e) -> p o u e", o=1, u=2).to_broadcast([P, 256, 2, 2]),
                    op=ALU.mult,
                )

            def quant_x(c):
                s = slice(256 * (c % 2), 256 * (c % 2) + 256)
                nc.vector.quantize_mx(out=xq[c // 2][:, s].bitcast(FP8X4), scales=xs[c // 2][:, s], in_=xg[c][:].rearrange("p r t -> p (r t)"))

            def perm_w():
                nc.vector.tensor_copy(
                    out=w1_perm[:].rearrange("p (t m b) -> p t m b", t=4, b=2),
                    in_=w1_raw[:].rearrange("p (m t b) -> p t m b", t=4, b=2),
                )

            def perm_s(e):
                (nc.vector if e == "v" else nc.gpsimd).tensor_copy(
                    out=w1_sperm[:].rearrange("p (t m) -> p t m", t=4),
                    in_=w1_sraw[:].rearrange("p (m t) -> p t m", t=4),
                )

            def mm1(t, c):
                if ("m1", t // 2, c) not in T:
                    T["m1", t // 2, c] = bank(2 * c + t // 2)
                nc.tensor.matmul_mx(
                    out=T["m1", t // 2, c][:, 256 * (t % 2) : 256 * (t % 2) + 256],
                    lhsT=w1_perm[:, 256 * t : 256 * t + 256].bitcast(FP4X4),
                    lhsT_scale=w1_sperm[:, 128 * t : 128 * t + 128],
                    rhs=xq[c // 2][:, 256 * (c % 2) : 256 * (c % 2) + 256].bitcast(FP8X4),
                    rhs_scale=xs[c // 2][:, 256 * (c % 2) : 256 * (c % 2) + 256],
                    start=True,
                    stop=True,
                )

            def bias1(t, c):
                nc.scalar.activation(
                    out=v1[c][:, t, :], in_=T["m1", t // 2, c][:, 256 * (t % 2) : 256 * (t % 2) + 256], func=ACT.Identity, bias=b1_col[:, t : t + 1]
                )

            def leaky1d(c):
                v = v1[c][:].rearrange("p t r -> p r t")
                nc.vector.scalar_tensor_tensor(out=h1[c][:], in0=v, scalar=SLOPE, in1=v, op0=ALU.mult, op1=ALU.max)

            def quant_h(c):
                s = slice(256 * (c % 2), 256 * (c % 2) + 256)
                nc.vector.quantize_mx(out=hq[c // 2][:, s].bitcast(FP8X4), scales=hs[c // 2][:, s], in_=h1[c][:].rearrange("p r t -> p (r t)"))

            def vec_turn():
                T["vec"] = bank(4, BF16, 1024)
                nc.tensor.transpose(T["vec"][:, 0:128], crow[:], identb[:])

            def vec_copy():
                nc.vector.tensor_copy(out=cst[:], in_=T["vec"][:, 0:12])
                nc.gpsimd.tensor_scalar(out=b2s[:], in0=cst[:, 0:4], scalar1=SLOPE, scalar2=0.0, op0=ALU.mult, op1=ALU.add)

            def mm2(j, h):
                b = bank(4 * h + j)
                nc.tensor.matmul_mx(
                    out=b[:],
                    lhsT=w2_raw[:, 256 * j : 256 * j + 256].bitcast(FP4X4),
                    lhsT_scale=w2_s[:, 128 * j : 128 * j + 128],
                    rhs=hq[h][:].bitcast(FP8X4),
                    rhs_scale=hs[h][:],
                    start=True,
                    stop=True,
                )
                T["m2", j, h] = b

            def low2(j, h):
                nc.scalar.activation(out=cc[j][h][:], in_=T["m2", j, h][:], func=ACT.Identity, bias=b2s[:, j : j + 1], scale=SLOPE)

            def leaky2(j, h):
                nc.vector.scalar_tensor_tensor(
                    out=h2[j][:, HALF * h : HALF * h + HALF], in0=T["m2", j, h][:], scalar=cst[:, j : j + 1], in1=cc[j][h][:], op0=ALU.add, op1=ALU.max, accum_out=acc[j][h][:]
                )

            def mean(j):
                nc.gpsimd.tensor_scalar(out=nmean[j][:], in0=acc[j][0][:], scalar1=acc[j][1][:], scalar2=-1.0 / NQ, op0=ALU.add, op1=ALU.mult)

            def square(j):
                nc.scalar.activation(out=junk[:], in_=h2[j][:], func=ACT.Square, bias=nmean[j][:], accum_out=ssq[j][:])

            def rstd_s(j):
                nc.scalar.activation(out=rstd[j][:], in_=ssq[j][:], func=ACT.Abs_reciprocal_sqrt, bias=EPS, scale=1.0 / NQ)

            def gain(j, e):
                (nc.vector if e == "v" else nc.gpsimd).tensor_tensor(out=scl[j][:], in0=rstd[j][:], in1=cst[:, 4 + j : 5 + j], op=ALU.mult)

            def shift(j, e):
                (nc.vector if e == "v" else nc.gpsimd).tensor_scalar(out=shf[j][:], in0=nmean[j][:], scalar1=scl[j][:], scalar2=cst[:, 8 + j : 9 + j], op0=ALU.mult, op1=ALU.add)

            def norm(j, g, e):
                lo, hi = 512 * g, 512 * g + 512
                if e == "s":
                    nc.scalar.activation(out=y2[j][:, lo:hi], in_=h2[j][:, lo:hi], func=ACT.Identity, scale=scl[j][:], bias=shf[j][:])
                else:
                    (nc.vector if e == "v" else nc.gpsimd).tensor_scalar(out=y2[j][:, lo:hi], in0=h2[j][:, lo:hi], scalar1=scl[j][:], scalar2=shf[j][:], op0=ALU.mult, op1=ALU.add)

            def flip(a, q):
                b = bank((2 * a, 2 * a + 1, 4 + 2 * a, 5 + 2 * a)[q])
                for i in range(2):
                    for n in range(2):
                        c0 = 128 * (2 * q + i)
                        nc.tensor.transpose(b[:, 256 * i + 128 * n : 256 * i + 128 * n + 128], y2[2 * a + n][:, c0 : c0 + 128], ident[:])
                T["f", a, q] = b

            def drain(a, q, e):
                (nc.vector.tensor_copy if e == "v" else nc.scalar.copy)(out=ot[a][q][:].rearrange("p i n -> p (i n)"), in_=T["f", a, q][:])

            def store(a, q):
                nc.sync.dma_start(out=out_v[:, 2 * q : 2 * q + 2, 256 * a : 256 * a + 256], in_=ot[a][q][:])


            widen(0, "v")
            widen(1, "s")
            turn(0)
            perm_w()
            widen(2, "s")
            widen(3, "s")
            turn(1)
            scale_x(0)
            perm_s("v")
            quant_x(0)
            scale_x(1)
            widen(6, "s")
            widen(7, "s")
            turn(3)
            widen(4, "s")
            mm1(2, 0)
            widen(5, "s")
            turn(2)
            mm1(3, 0)
            bias1(3, 0)
            scale_x(3)
            quant_x(1)
            mm1(0, 0)
            mm1(1, 0)
            bias1(1, 0)
            mm1(3, 1)
            scale_x(2)
            mm1(2, 1)
            bias1(0, 0)
            mm1(0, 1)
            mm1(1, 1)
            vec_turn()
            quant_x(3)
            bias1(2, 0)
            mm1(2, 3)
            quant_x(2)
            vec_copy()
            mm1(3, 2)
            leaky1d(0)
            bias1(0, 1)
            bias1(2, 1)
            mm1(0, 2)
            mm1(1, 3)
            bias1(1, 1)
            bias1(3, 1)
            leaky1d(1)
            mm1(1, 2)
            bias1(1, 2)
            bias1(0, 2)
            mm1(2, 2)
            bias1(2, 2)
            mm1(0, 3)
            quant_h(0)
            bias1(1, 3)
            quant_h(1)
            bias1(3, 2)
            bias1(0, 3)
            leaky1d(2)
            mm1(3, 3)
            mm2(2, 0)
            bias1(3, 3)
            bias1(2, 3)
            low2(2, 0)
            leaky1d(3)
            quant_h(2)
            quant_h(3)
            mm2(0, 0)
            mm2(1, 0)
            leaky2(2, 0)
            low2(0, 0)
            leaky2(0, 0)
            mm2(3, 0)
            low2(3, 0)
            low2(1, 0)
            leaky2(1, 0)
            mm2(0, 1)
            low2(0, 1)
            mm2(3, 1)
            leaky2(0, 1)
            mm2(2, 1)
            low2(3, 1)
            mm2(1, 1)
            low2(2, 1)
            mean(0)
            leaky2(3, 1)
            low2(1, 1)
            square(0)
            leaky2(1, 1)
            mean(1)
            leaky2(2, 1)
            rstd_s(0)
            gain(0, "g")
            mean(2)
            leaky2(3, 0)
            square(1)
            shift(0, "g")
            rstd_s(1)
            gain(1, "v")
            norm(0, 0, "g")
            mean(3)
            shift(1, "v")
            norm(1, 0, "v")
            flip(0, 0)
            norm(1, 1, "v")
            square(2)
            rstd_s(2)
            flip(0, 1)
            gain(2, "g")
            norm(0, 1, "v")
            drain(0, 0, "v")
            store(0, 0)
            drain(0, 1, "v")
            square(3)
            rstd_s(3)
            gain(3, "v")
            store(0, 1)
            shift(3, "v")
            flip(0, 2)
            drain(0, 2, "s")
            norm(3, 0, "v")
            shift(2, "g")
            norm(2, 0, "g")
            store(0, 2)
            norm(2, 1, "v")
            norm(3, 1, "v")
            flip(0, 3)
            flip(1, 0)
            drain(1, 0, "v")
            flip(1, 3)
            drain(1, 3, "v")
            drain(0, 3, "s")
            store(0, 3)
            flip(1, 2)
            drain(1, 2, "v")
            store(1, 0)
            store(1, 3)
            store(1, 2)
            flip(1, 1)
            drain(1, 1, "s")
            store(1, 1)
